import numpy as np
import ml_dtypes


def mxq(x, axis, fmt="e4m3"):
    dtype, down = {"e4m3": (ml_dtypes.float8_e4m3fn, 7), "e5m2": (ml_dtypes.float8_e5m2, 14)}[fmt]
    v = np.moveaxis(np.asarray(x, np.float32).astype(ml_dtypes.bfloat16).astype(np.float64), axis, -1)
    blocks = v.reshape(v.shape[:-1] + (-1, 32))
    amax = np.abs(blocks).max(-1, keepdims=True)
    byte = np.maximum(np.where(amax > 0, np.frexp(amax)[1] - 1 + 127, 0) - down, 1)
    scale = np.exp2(byte - 127.0)
    codes = (blocks / scale).astype(np.float32).astype(dtype).astype(np.float64)
    return np.moveaxis((codes * scale).reshape(v.shape), -1, axis)


WIDE = False


def mx_kscale(k):
    if not WIDE:
        return np.ones(k)
    levels = np.array([10, -10, 5, -5, 0])
    a = np.random.permutation(np.resize(levels, k // 512 * 4)).reshape(k // 512, 4)
    idx = np.arange(k)
    return np.exp2(a[idx // 512, idx % 128 // 32])


BF16 = ml_dtypes.bfloat16


def bf(x):
    return np.asarray(x, np.float32).astype(BF16)


def f64(x):
    return np.asarray(x).astype(np.float64)


E2M1 = np.array([0.0, 0.5, 1.0, 1.5, 2.0, 3.0, 4.0, 6.0, -0.0, -0.5, -1.0, -1.5, -2.0, -3.0, -4.0, -6.0])


def pack_weight(w, fmt):
    k, n = w.shape
    w = f64(bf(w)).reshape(k // 32, 32, n)
    amax = np.abs(w).max(1)
    if fmt == "e4m3":
        byte = np.frexp(amax)[1] - 1 + 127 - 7
    else:
        mant, ex = np.frexp(amax / 6.0)
        byte = np.where(mant > 0.5, ex, ex - 1) + 127
    byte = np.clip(np.where(amax > 0, byte, 1), 1, 254)
    scaled = (w * np.exp2(127.0 - byte)[:, None, :]).reshape(k, n).astype(np.float32)
    by_word = np.ascontiguousarray(scaled.reshape(k // 512, 128, 4, n).transpose(0, 1, 3, 2))
    if fmt == "e4m3":
        words = by_word.astype(ml_dtypes.float8_e4m3fn).view(np.uint8)
    else:
        c = by_word.astype(ml_dtypes.float4_e2m1fn).view(np.uint8) & 0xF
        words = c[..., 0::2] | (c[..., 1::2] << 4)
    return np.ascontiguousarray(words), np.ascontiguousarray(byte.astype(np.uint8).reshape(k // 512, 16, n))


def unpack_weight(words, scales, fmt):
    g, p, n, _ = words.shape
    if fmt == "e4m3":
        vals = np.ascontiguousarray(words).view(ml_dtypes.float8_e4m3fn).astype(np.float64)
    else:
        nib = np.empty((g, p, n, 4), np.uint8)
        nib[..., 0::2] = words & 0xF
        nib[..., 1::2] = words >> 4
        vals = E2M1[nib]
    vals = vals * np.repeat(np.exp2(scales.astype(np.float64) - 127.0), 8, axis=1)[..., None]
    return vals.transpose(0, 1, 3, 2).reshape(g * 512, n)

def pack4(w):
    words, scales = pack_weight(w, "e2m1")
    return words.reshape(words.shape[0], 128, -1), scales


def unpack4(words, scales):
    return unpack_weight(words.reshape(words.shape[0], 128, -1, 2), scales, "e2m1")


B, N, D, A = 4, 4096, 256, 128
K = D + D
NB = N // A


def setup_inputs():
    st = mx_kscale(K)
    s, t = st[:D], st[D:]
    data = bf(np.random.standard_normal((B, N, D)) * 2.0 * s)
    pooled = bf(np.random.standard_normal((B, N, A)) * 0.37 / np.sqrt(NB))
    W_abs = bf(np.random.standard_normal((A, D)) * 3.0 * np.sqrt(NB / A) * t)
    words, scales = pack4(np.random.standard_normal((K, D)) * 0.5 / np.sqrt(D) / st[:, None])
    return {"data": data,
            "pooled": pooled,
            "W_abs": W_abs,
            "W_merge_words": words,
            "W_merge_scales": scales}


def reference(data, pooled, W_abs, W_merge_words, W_merge_scales):
    abstract = f64(pooled) @ f64(W_abs)
    x = np.concatenate([f64(data), abstract], axis=-1)
    return mxq(x, 2, "e4m3") @ unpack4(W_merge_words, W_merge_scales)

@@ -1,0 +1,188 @@
+from contextlib import ExitStack
+
+import concourse.mybir as mybir
+from concourse.masks import make_identity
+
+BF16 = mybir.dt.bfloat16
+F32 = mybir.dt.float32
+I32 = mybir.dt.int32
+U8 = mybir.dt.uint8
+U32 = mybir.dt.uint32
+FP8X4 = mybir.dt.float8_e4m3fn_x4
+FP4X4 = mybir.dt.float4_e2m1fn_x4
+
+P = 128
+TOKENS = 4 * 4096
+D = 256
+A = 128
+HALF = D // 4
+PLANES = 2
+J = 8
+N_CHUNKS = TOKENS // (P * J)
+GROUP = 4
+N_GROUPS = TOKENS // (P * GROUP)
+GROUPS_PER_CHUNK = J // GROUP
+PER_BANK = 2
+
+FLOPS = 2 * TOKENS * A * D + 2 * TOKENS * (2 * D) * D
+
+
+def tile_abstraction_pb_t_kernel(tc, data, pooled, W_abs, W_merge_words, W_merge_scales, out):
+    nc = tc.nc
+    data_chunks = data.flatten_outer_dims().rearrange("(c p j) d -> c p j d", p=P, j=J)
+    pooled_chunks = pooled.flatten_outer_dims().rearrange("(c p j) a -> c p j a", p=P, j=J)
+    out_chunks = out.flatten_outer_dims().rearrange("(c p j) n -> c p j n", p=P, j=J)
+
+    with ExitStack() as ctx:
+        ctx.enter_context(tc.manual_schedule())
+        consts = ctx.enter_context(tc.tile_pool(name="consts", bufs=1))
+        inputs = ctx.enter_context(tc.tile_pool(name="inputs", bufs=1))
+        pooled_t_pool = ctx.enter_context(tc.tile_pool(name="pooled_t", bufs=3))
+        x_pool = ctx.enter_context(tc.tile_pool(name="x", bufs=4))
+        grouped_pool = ctx.enter_context(tc.tile_pool(name="grouped", bufs=3))
+        codes_pool = ctx.enter_context(tc.tile_pool(name="codes", bufs=3))
+        out_pool = ctx.enter_context(tc.tile_pool(name="out", bufs=8))
+        psum_pooled_t = ctx.enter_context(tc.psum_pool(name="psum_pooled_t", bufs=1))
+        psum_abstract = ctx.enter_context(tc.psum_pool(name="psum_abstract", bufs=1))
+        psum_x_t = ctx.enter_context(tc.psum_pool(name="psum_x_t", bufs=3))
+        psum_out = ctx.enter_context(tc.psum_pool(name="psum_out", bufs=3))
+
+        ident_bf16 = consts.tile([P, P], BF16)
+        make_identity(nc, ident_bf16[:])
+        ident_f32 = consts.tile([P, P], F32)
+        make_identity(nc, ident_f32[:])
+        w_scales = consts.tile([P, D], U8, align_bytes=64)
+        nc.vector.memset(w_scales[:].bitcast(I32), 0)
+
+        data_sb = {}
+        pooled_sb = {}
+
+        def load_chunk(c):
+            pooled_c = inputs.tile([P, J, A], BF16, name="pooled%d" % c)
+            nc.sync.dma_start(out=pooled_c[:], in_=pooled_chunks[c])
+            pooled_sb[c] = pooled_c
+            data_c = inputs.tile([P, J, D], BF16, name="data%d" % c)
+            nc.sync.dma_start(out=data_c[:], in_=data_chunks[c])
+            data_sb[c] = data_c
+
+        w_abs_raw = consts.tile([A, D], BF16)
+        nc.sync.dma_start(out=w_abs_raw[:], in_=W_abs)
+        load_chunk(0)
+        w_words = consts.tile([P, 2 * D], U8, align_bytes=64)
+        nc.sync.dma_start(out=w_words[:].bitcast(I32), in_=W_merge_words[0].bitcast(I32))
+        for quadrant in range(4):
+            nc.sync.dma_start(
+                out=w_scales[32 * quadrant : 32 * quadrant + 4, :].bitcast(I32),
+                in_=W_merge_scales[0, 4 * quadrant : 4 * quadrant + 4, :].bitcast(I32),
+            )
+        for c in range(1, N_CHUNKS):
+            load_chunk(c)
+
+        w_abs = consts.tile([A, PLANES, HALF, 2], BF16)
+        nc.vector.tensor_copy(
+            out=w_abs[:].bitcast(F32),
+            in_=w_abs_raw[:].bitcast(F32).rearrange("a (i u) -> a u i", u=PLANES).unsqueeze(3),
+        )
+
+        pooled_t_sb = {}
+        x_sb = {}
+        grouped_sb = {}
+        codes_sb = {}
+        scales_sb = {}
+        out_sb = {}
+
+        def chunk_and_first_tile(g):
+            return g // GROUPS_PER_CHUNK, GROUP * (g % GROUPS_PER_CHUNK)
+
+        def transpose_pooled(g):
+            c, j0 = chunk_and_first_tile(g)
+            pooled_t_ps = psum_pooled_t.tile([A, GROUP, P], BF16)
+            for j in range(GROUP):
+                nc.tensor.transpose(pooled_t_ps[:, j, :], pooled_sb[c][:, j0 + j, :], ident_bf16[:])
+            pooled_t = pooled_t_pool.tile([A, GROUP, P], BF16)
+            nc.scalar.copy(out=pooled_t[:], in_=pooled_t_ps[:])
+            pooled_t_sb[g] = pooled_t
+
+        def sort_data(g):
+            c, j0 = chunk_and_first_tile(g)
+            x = x_pool.tile([P, GROUP, PLANES, 2 * P], BF16)
+            nc.vector.tensor_copy(
+                out=x[:].bitcast(F32)[:, :, :, 0:HALF],
+                in_=data_sb[c][:].bitcast(F32)[:, j0 : j0 + GROUP, :].rearrange("p j (i u) -> p j u i", u=PLANES),
+            )
+            x_sb[g] = x
+
+        def abstract(g):
+            abstract_ps = psum_abstract.tile([P, GROUP, PLANES, 2 * HALF], BF16)
+            for j in range(GROUP):
+                nc.tensor.matmul(
+                    out=abstract_ps[:, j, :, :].rearrange("p u w -> p (u w)"),
+                    lhsT=pooled_t_sb[g][:, j, :],
+                    rhs=w_abs[:].rearrange("a u i e -> a (u i e)"),
+                    start=True,
+                    stop=True,
+                )
+            nc.scalar.copy(out=x_sb[g][:, :, :, 2 * HALF : 4 * HALF], in_=abstract_ps[:])
+
+        def transpose_x(g):
+            grouped = grouped_pool.tile([P, GROUP, P, 4], BF16, align_bytes=64)
+            for half in range(GROUP // PER_BANK):
+                x_t_ps = psum_x_t.tile([P, PER_BANK, PLANES, P], F32)
+                for j in range(PER_BANK):
+                    for u in range(PLANES):
+                        nc.tensor.transpose(
+                            x_t_ps[:, j, u, :],
+                            x_sb[g][:].bitcast(F32)[:, PER_BANK * half + j, u, :],
+                            ident_f32[:],
+                        )
+                nc.vector.tensor_copy(
+                    out=grouped[:].bitcast(F32)[:, PER_BANK * half : PER_BANK * (half + 1), :, :],
+                    in_=x_t_ps[:].rearrange("p j u r -> p j r u"),
+                )
+            grouped_sb[g] = grouped
+
+        def quantise(g):
+            codes = codes_pool.tile([P, GROUP * P], U32, align_bytes=64)
+            scales = codes_pool.tile([P, GROUP * P], U8, align_bytes=64)
+            nc.vector.quantize_mx(
+                out=codes[:].bitcast(FP8X4),
+                scales=scales[:],
+                in_=grouped_sb[g][:].rearrange("p j r t -> p (j r t)"),
+            )
+            codes_sb[g] = codes
+            scales_sb[g] = scales
+
+        def merge(g):
+            c, j0 = chunk_and_first_tile(g)
+            if j0 == 0:
+                out_c = out_pool.tile([P, J, D], F32)
+                out_sb[c] = out_c
+            for half in range(GROUP // PER_BANK):
+                out_ps = psum_out.tile([P, PER_BANK, D], F32)
+                for j in range(PER_BANK):
+                    tokens = slice(P * (PER_BANK * half + j), P * (PER_BANK * half + j + 1))
+                    nc.tensor.matmul_mx(
+                        out=out_ps[:, j, :],
+                        lhsT=codes_sb[g][:, tokens].bitcast(FP8X4),
+                        lhsT_scale=scales_sb[g][:, tokens],
+                        rhs=w_words[:].bitcast(FP4X4),
+                        rhs_scale=w_scales[:],
+                        start=True,
+                        stop=True,
+                    )
+                first = j0 + PER_BANK * half
+                nc.scalar.copy(out=out_sb[c][:, first : first + PER_BANK, :], in_=out_ps[:])
+            if j0 + GROUP == J:
+                nc.sync.dma_start(out=out_chunks[c], in_=out_sb[c][:])
+
+        def run(stage, g):
+            if 0 <= g < N_GROUPS:
+                stage(g)
+
+        for step in range(N_GROUPS + 4):
+            run(merge, step - 4)
+            run(abstract, step - 1)
+            run(sort_data, step)
+            run(transpose_pooled, step)
+            run(quantise, step - 3)
+            run(transpose_x, step - 2)

@@ -37,11 +37,11 @@ def tile_abstraction_pb_t_kernel(tc, data, pooled, W_abs, W_merge_words, W_merge
         ctx.enter_context(tc.manual_schedule())
         consts = ctx.enter_context(tc.tile_pool(name="consts", bufs=1))
         inputs = ctx.enter_context(tc.tile_pool(name="inputs", bufs=1))
-        pooled_t_pool = ctx.enter_context(tc.tile_pool(name="pooled_t", bufs=3))
+        pooled_t_pool = ctx.enter_context(tc.tile_pool(name="pooled_t", bufs=4))
         x_pool = ctx.enter_context(tc.tile_pool(name="x", bufs=4))
         grouped_pool = ctx.enter_context(tc.tile_pool(name="grouped", bufs=3))
         codes_pool = ctx.enter_context(tc.tile_pool(name="codes", bufs=3))
-        out_pool = ctx.enter_context(tc.tile_pool(name="out", bufs=8))
+        out_pool = ctx.enter_context(tc.tile_pool(name="out", bufs=16))
         psum_pooled_t = ctx.enter_context(tc.psum_pool(name="psum_pooled_t", bufs=1))
         psum_abstract = ctx.enter_context(tc.psum_pool(name="psum_abstract", bufs=1))
         psum_x_t = ctx.enter_context(tc.psum_pool(name="psum_x_t", bufs=3))
@@ -89,19 +89,12 @@ def tile_abstraction_pb_t_kernel(tc, data, pooled, W_abs, W_merge_words, W_merge
         grouped_sb = {}
         codes_sb = {}
         scales_sb = {}
-        out_sb = {}
+
+        def in_range(g):
+            return 0 <= g < N_GROUPS
 
         def chunk_and_first_tile(g):
             return g // GROUPS_PER_CHUNK, GROUP * (g % GROUPS_PER_CHUNK)
-
-        def transpose_pooled(g):
-            c, j0 = chunk_and_first_tile(g)
-            pooled_t_ps = psum_pooled_t.tile([A, GROUP, P], BF16)
-            for j in range(GROUP):
-                nc.tensor.transpose(pooled_t_ps[:, j, :], pooled_sb[c][:, j0 + j, :], ident_bf16[:])
-            pooled_t = pooled_t_pool.tile([A, GROUP, P], BF16)
-            nc.scalar.copy(out=pooled_t[:], in_=pooled_t_ps[:])
-            pooled_t_sb[g] = pooled_t
 
         def sort_data(g):
             c, j0 = chunk_and_first_tile(g)
@@ -112,17 +105,29 @@ def tile_abstraction_pb_t_kernel(tc, data, pooled, W_abs, W_merge_words, W_merge
             )
             x_sb[g] = x
 
-        def abstract(g):
-            abstract_ps = psum_abstract.tile([P, GROUP, PLANES, 2 * HALF], BF16)
+        def abstract_and_pooled_t(g_abstract, g_pooled):
+            if in_range(g_abstract):
+                abstract_ps = psum_abstract.tile([P, GROUP, PLANES, 2 * HALF], BF16)
+            if in_range(g_pooled):
+                c, j0 = chunk_and_first_tile(g_pooled)
+                pooled_t_ps = psum_pooled_t.tile([A, GROUP, P], BF16)
             for j in range(GROUP):
-                nc.tensor.matmul(
-                    out=abstract_ps[:, j, :, :].rearrange("p u w -> p (u w)"),
-                    lhsT=pooled_t_sb[g][:, j, :],
-                    rhs=w_abs[:].rearrange("a u i e -> a (u i e)"),
-                    start=True,
-                    stop=True,
-                )
-            nc.scalar.copy(out=x_sb[g][:, :, :, 2 * HALF : 4 * HALF], in_=abstract_ps[:])
+                if in_range(g_abstract):
+                    nc.tensor.matmul(
+                        out=abstract_ps[:, j, :, :].rearrange("p u w -> p (u w)"),
+                        lhsT=pooled_t_sb[g_abstract][:, j, :],
+                        rhs=w_abs[:].rearrange("a u i e -> a (u i e)"),
+                        start=True,
+                        stop=True,
+                    )
+                if in_range(g_pooled):
+                    nc.tensor.transpose(pooled_t_ps[:, j, :], pooled_sb[c][:, j0 + j, :], ident_bf16[:])
+            if in_range(g_abstract):
+                nc.scalar.copy(out=x_sb[g_abstract][:, :, :, 2 * HALF : 4 * HALF], in_=abstract_ps[:])
+            if in_range(g_pooled):
+                pooled_t = pooled_t_pool.tile([A, GROUP, P], BF16)
+                nc.scalar.copy(out=pooled_t[:], in_=pooled_t_ps[:])
+                pooled_t_sb[g_pooled] = pooled_t
 
         def transpose_x(g):
             grouped = grouped_pool.tile([P, GROUP, P, 4], BF16, align_bytes=64)
@@ -154,9 +159,7 @@ def tile_abstraction_pb_t_kernel(tc, data, pooled, W_abs, W_merge_words, W_merge
 
         def merge(g):
             c, j0 = chunk_and_first_tile(g)
-            if j0 == 0:
-                out_c = out_pool.tile([P, J, D], F32)
-                out_sb[c] = out_c
+            out_g = out_pool.tile([P, GROUP, D], F32)
             for half in range(GROUP // PER_BANK):
                 out_ps = psum_out.tile([P, PER_BANK, D], F32)
                 for j in range(PER_BANK):
@@ -170,19 +173,16 @@ def tile_abstraction_pb_t_kernel(tc, data, pooled, W_abs, W_merge_words, W_merge
                         start=True,
                         stop=True,
                     )
-                first = j0 + PER_BANK * half
-                nc.scalar.copy(out=out_sb[c][:, first : first + PER_BANK, :], in_=out_ps[:])
-            if j0 + GROUP == J:
-                nc.sync.dma_start(out=out_chunks[c], in_=out_sb[c][:])
+                nc.scalar.copy(out=out_g[:, PER_BANK * half : PER_BANK * (half + 1), :], in_=out_ps[:])
+            nc.sync.dma_start(out=out_chunks[c, :, j0 : j0 + GROUP, :], in_=out_g[:])
 
-        def run(stage, g):
-            if 0 <= g < N_GROUPS:
-                stage(g)
-
-        for step in range(N_GROUPS + 4):
-            run(merge, step - 4)
-            run(abstract, step - 1)
-            run(sort_data, step)
-            run(transpose_pooled, step)
-            run(quantise, step - 3)
-            run(transpose_x, step - 2)
+        for step in range(N_GROUPS + 5):
+            if in_range(step - 5):
+                merge(step - 5)
+            abstract_and_pooled_t(step - 2, step)
+            if in_range(step - 1):
+                sort_data(step - 1)
+            if in_range(step - 4):
+                quantise(step - 4)
+            if in_range(step - 3):
+                transpose_x(step - 3)

@@ -23,6 +23,11 @@ GROUP = 4
 N_GROUPS = TOKENS // (P * GROUP)
 GROUPS_PER_CHUNK = J // GROUP
 PER_BANK = 2
+SORT_LAG = 1
+ABSTRACT_LAG = 2
+TRANSPOSE_LAG = 3
+QUANTISE_LAG = 4
+MERGE_LAG = 6
 
 FLOPS = 2 * TOKENS * A * D + 2 * TOKENS * (2 * D) * D
 
@@ -40,11 +45,11 @@ def tile_abstraction_pb_t_kernel(tc, data, pooled, W_abs, W_merge_words, W_merge
         pooled_t_pool = ctx.enter_context(tc.tile_pool(name="pooled_t", bufs=4))
         x_pool = ctx.enter_context(tc.tile_pool(name="x", bufs=4))
         grouped_pool = ctx.enter_context(tc.tile_pool(name="grouped", bufs=3))
-        codes_pool = ctx.enter_context(tc.tile_pool(name="codes", bufs=3))
+        codes_pool = ctx.enter_context(tc.tile_pool(name="codes", bufs=4))
         out_pool = ctx.enter_context(tc.tile_pool(name="out", bufs=16))
         psum_pooled_t = ctx.enter_context(tc.psum_pool(name="psum_pooled_t", bufs=1))
-        psum_abstract = ctx.enter_context(tc.psum_pool(name="psum_abstract", bufs=1))
-        psum_x_t = ctx.enter_context(tc.psum_pool(name="psum_x_t", bufs=3))
+        psum_abstract = ctx.enter_context(tc.psum_pool(name="psum_abstract", bufs=2))
+        psum_x_t = ctx.enter_context(tc.psum_pool(name="psum_x_t", bufs=2))
         psum_out = ctx.enter_context(tc.psum_pool(name="psum_out", bufs=3))
 
         ident_bf16 = consts.tile([P, P], BF16)
@@ -84,105 +89,122 @@ def tile_abstraction_pb_t_kernel(tc, data, pooled, W_abs, W_merge_words, W_merge
             in_=w_abs_raw[:].bitcast(F32).rearrange("a (i u) -> a u i", u=PLANES).unsqueeze(3),
         )
 
+        pooled_t_ps = {}
         pooled_t_sb = {}
         x_sb = {}
+        abstract_ps = {}
+        x_t_ps = {}
         grouped_sb = {}
         codes_sb = {}
         scales_sb = {}
-
-        def in_range(g):
-            return 0 <= g < N_GROUPS
+        out_ps = {}
+        out_sb = {}
 
         def chunk_and_first_tile(g):
             return g // GROUPS_PER_CHUNK, GROUP * (g % GROUPS_PER_CHUNK)
 
+        def transpose_pooled(g):
+            c, j0 = chunk_and_first_tile(g)
+            pooled_t_ps[g] = psum_pooled_t.tile([A, GROUP, P], BF16, name="pooled_t_ps")
+            for j in range(GROUP):
+                nc.tensor.transpose(pooled_t_ps[g][:, j, :], pooled_sb[c][:, j0 + j, :], ident_bf16[:])
+            pooled_t_sb[g] = pooled_t_pool.tile([A, GROUP, P], BF16, name="pooled_t")
+            nc.scalar.copy(out=pooled_t_sb[g][:], in_=pooled_t_ps[g][:])
+
         def sort_data(g):
             c, j0 = chunk_and_first_tile(g)
-            x = x_pool.tile([P, GROUP, PLANES, 2 * P], BF16)
+            x_sb[g] = x_pool.tile([P, GROUP, PLANES, 2 * P], BF16, name="x")
             nc.vector.tensor_copy(
-                out=x[:].bitcast(F32)[:, :, :, 0:HALF],
+                out=x_sb[g][:].bitcast(F32)[:, :, :, 0:HALF],
                 in_=data_sb[c][:].bitcast(F32)[:, j0 : j0 + GROUP, :].rearrange("p j (i u) -> p j u i", u=PLANES),
             )
-            x_sb[g] = x
 
-        def abstract_and_pooled_t(g_abstract, g_pooled):
-            if in_range(g_abstract):
-                abstract_ps = psum_abstract.tile([P, GROUP, PLANES, 2 * HALF], BF16)
-            if in_range(g_pooled):
-                c, j0 = chunk_and_first_tile(g_pooled)
-                pooled_t_ps = psum_pooled_t.tile([A, GROUP, P], BF16)
-            for j in range(GROUP):
-                if in_range(g_abstract):
-                    nc.tensor.matmul(
-                        out=abstract_ps[:, j, :, :].rearrange("p u w -> p (u w)"),
-                        lhsT=pooled_t_sb[g_abstract][:, j, :],
-                        rhs=w_abs[:].rearrange("a u i e -> a (u i e)"),
-                        start=True,
-                        stop=True,
-                    )
-                if in_range(g_pooled):
-                    nc.tensor.transpose(pooled_t_ps[:, j, :], pooled_sb[c][:, j0 + j, :], ident_bf16[:])
-            if in_range(g_abstract):
-                nc.scalar.copy(out=x_sb[g_abstract][:, :, :, 2 * HALF : 4 * HALF], in_=abstract_ps[:])
-            if in_range(g_pooled):
-                pooled_t = pooled_t_pool.tile([A, GROUP, P], BF16)
-                nc.scalar.copy(out=pooled_t[:], in_=pooled_t_ps[:])
-                pooled_t_sb[g_pooled] = pooled_t
+        def abstract_matmuls(g, tiles):
+            if g not in abstract_ps:
+                abstract_ps[g] = psum_abstract.tile([P, GROUP, PLANES, 2 * HALF], BF16, name="abstract_ps")
+            for j in tiles:
+                nc.tensor.matmul(
+                    out=abstract_ps[g][:, j, :, :].rearrange("p u w -> p (u w)"),
+                    lhsT=pooled_t_sb[g][:, j, :],
+                    rhs=w_abs[:].rearrange("a u i e -> a (u i e)"),
+                    start=True,
+                    stop=True,
+                )
+
+        def abstract_to_x(g):
+            nc.scalar.copy(out=x_sb[g][:, :, :, 2 * HALF : 4 * HALF], in_=abstract_ps[g][:])
 
         def transpose_x(g):
-            grouped = grouped_pool.tile([P, GROUP, P, 4], BF16, align_bytes=64)
+            grouped_sb[g] = grouped_pool.tile([P, GROUP, P, 4], BF16, align_bytes=64, name="grouped")
             for half in range(GROUP // PER_BANK):
-                x_t_ps = psum_x_t.tile([P, PER_BANK, PLANES, P], F32)
+                x_t_ps[g] = psum_x_t.tile([P, PER_BANK, PLANES, P], F32, name="x_t_ps")
                 for j in range(PER_BANK):
                     for u in range(PLANES):
                         nc.tensor.transpose(
-                            x_t_ps[:, j, u, :],
+                            x_t_ps[g][:, j, u, :],
                             x_sb[g][:].bitcast(F32)[:, PER_BANK * half + j, u, :],
                             ident_f32[:],
                         )
                 nc.vector.tensor_copy(
-                    out=grouped[:].bitcast(F32)[:, PER_BANK * half : PER_BANK * (half + 1), :, :],
-                    in_=x_t_ps[:].rearrange("p j u r -> p j r u"),
+                    out=grouped_sb[g][:].bitcast(F32)[:, PER_BANK * half : PER_BANK * (half + 1), :, :],
+                    in_=x_t_ps[g][:].rearrange("p j u r -> p j r u"),
                 )
-            grouped_sb[g] = grouped
 
         def quantise(g):
-            codes = codes_pool.tile([P, GROUP * P], U32, align_bytes=64)
-            scales = codes_pool.tile([P, GROUP * P], U8, align_bytes=64)
+            codes_sb[g] = codes_pool.tile([P, GROUP * P], U32, align_bytes=64, name="codes")
+            scales_sb[g] = codes_pool.tile([P, GROUP * P], U8, align_bytes=64, name="scales")
             nc.vector.quantize_mx(
-                out=codes[:].bitcast(FP8X4),
-                scales=scales[:],
+                out=codes_sb[g][:].bitcast(FP8X4),
+                scales=scales_sb[g][:],
                 in_=grouped_sb[g][:].rearrange("p j r t -> p (j r t)"),
             )
-            codes_sb[g] = codes
-            scales_sb[g] = scales
 
-        def merge(g):
+        def merge_passes(g, half):
+            out_ps[g, half] = psum_out.tile([P, PER_BANK, D], F32, name="out_ps")
+            for j in range(PER_BANK):
+                tokens = slice(P * (PER_BANK * half + j), P * (PER_BANK * half + j + 1))
+                nc.tensor.matmul_mx(
+                    out=out_ps[g, half][:, j, :],
+                    lhsT=codes_sb[g][:, tokens].bitcast(FP8X4),
+                    lhsT_scale=scales_sb[g][:, tokens],
+                    rhs=w_words[:].bitcast(FP4X4),
+                    rhs_scale=w_scales[:],
+                    start=True,
+                    stop=True,
+                )
+
+        def out_of_psum(g, half):
+            if g not in out_sb:
+                out_sb[g] = out_pool.tile([P, GROUP, D], F32, name="out_g")
+            nc.scalar.copy(out=out_sb[g][:, PER_BANK * half : PER_BANK * (half + 1), :], in_=out_ps[g, half][:])
+
+        def store(g):
             c, j0 = chunk_and_first_tile(g)
-            out_g = out_pool.tile([P, GROUP, D], F32)
-            for half in range(GROUP // PER_BANK):
-                out_ps = psum_out.tile([P, PER_BANK, D], F32)
-                for j in range(PER_BANK):
-                    tokens = slice(P * (PER_BANK * half + j), P * (PER_BANK * half + j + 1))
-                    nc.tensor.matmul_mx(
-                        out=out_ps[:, j, :],
-                        lhsT=codes_sb[g][:, tokens].bitcast(FP8X4),
-                        lhsT_scale=scales_sb[g][:, tokens],
-                        rhs=w_words[:].bitcast(FP4X4),
-                        rhs_scale=w_scales[:],
-                        start=True,
-                        stop=True,
-                    )
-                nc.scalar.copy(out=out_g[:, PER_BANK * half : PER_BANK * (half + 1), :], in_=out_ps[:])
-            nc.sync.dma_start(out=out_chunks[c, :, j0 : j0 + GROUP, :], in_=out_g[:])
+            nc.sync.dma_start(out=out_chunks[c, :, j0 : j0 + GROUP, :], in_=out_sb[g][:])
 
-        for step in range(N_GROUPS + 5):
-            if in_range(step - 5):
-                merge(step - 5)
-            abstract_and_pooled_t(step - 2, step)
-            if in_range(step - 1):
-                sort_data(step - 1)
-            if in_range(step - 4):
-                quantise(step - 4)
-            if in_range(step - 3):
-                transpose_x(step - 3)
+        def in_range(g):
+            return 0 <= g < N_GROUPS
+
+        for step in range(N_GROUPS + MERGE_LAG):
+            g_abstract = step - ABSTRACT_LAG
+            g_merge = step - MERGE_LAG
+            if in_range(g_abstract):
+                abstract_matmuls(g_abstract, (0, 1))
+            if in_range(g_merge):
+                merge_passes(g_merge, 0)
+                out_of_psum(g_merge, 0)
+                merge_passes(g_merge, 1)
+            if in_range(g_abstract):
+                abstract_matmuls(g_abstract, (2, 3))
+                abstract_to_x(g_abstract)
+            if in_range(g_merge):
+                out_of_psum(g_merge, 1)
+                store(g_merge)
+            if in_range(step - SORT_LAG):
+                sort_data(step - SORT_LAG)
+            if in_range(step - QUANTISE_LAG):
+                quantise(step - QUANTISE_LAG)
+            if in_range(step - TRANSPOSE_LAG):
+                transpose_x(step - TRANSPOSE_LAG)
+            if in_range(step):
+                transpose_pooled(step)

@@ -23,6 +23,7 @@ GROUP = 4
 N_GROUPS = TOKENS // (P * GROUP)
 GROUPS_PER_CHUNK = J // GROUP
 PER_BANK = 2
+PSUM_BANKS = 8
 SORT_LAG = 1
 ABSTRACT_LAG = 2
 TRANSPOSE_LAG = 3
@@ -47,10 +48,7 @@ def tile_abstraction_pb_t_kernel(tc, data, pooled, W_abs, W_merge_words, W_merge
         grouped_pool = ctx.enter_context(tc.tile_pool(name="grouped", bufs=3))
         codes_pool = ctx.enter_context(tc.tile_pool(name="codes", bufs=4))
         out_pool = ctx.enter_context(tc.tile_pool(name="out", bufs=16))
-        psum_pooled_t = ctx.enter_context(tc.psum_pool(name="psum_pooled_t", bufs=1))
-        psum_abstract = ctx.enter_context(tc.psum_pool(name="psum_abstract", bufs=2))
-        psum_x_t = ctx.enter_context(tc.psum_pool(name="psum_x_t", bufs=2))
-        psum_out = ctx.enter_context(tc.psum_pool(name="psum_out", bufs=3))
+        psum = ctx.enter_context(tc.psum_pool(name="psum", bufs=PSUM_BANKS))
 
         ident_bf16 = consts.tile([P, P], BF16)
         make_identity(nc, ident_bf16[:])
@@ -105,7 +103,7 @@ def tile_abstraction_pb_t_kernel(tc, data, pooled, W_abs, W_merge_words, W_merge
 
         def transpose_pooled(g):
             c, j0 = chunk_and_first_tile(g)
-            pooled_t_ps[g] = psum_pooled_t.tile([A, GROUP, P], BF16, name="pooled_t_ps")
+            pooled_t_ps[g] = psum.tile([A, GROUP, P], BF16, name="bank")
             for j in range(GROUP):
                 nc.tensor.transpose(pooled_t_ps[g][:, j, :], pooled_sb[c][:, j0 + j, :], ident_bf16[:])
             pooled_t_sb[g] = pooled_t_pool.tile([A, GROUP, P], BF16, name="pooled_t")
@@ -121,7 +119,7 @@ def tile_abstraction_pb_t_kernel(tc, data, pooled, W_abs, W_merge_words, W_merge
 
         def abstract_matmuls(g, tiles):
             if g not in abstract_ps:
-                abstract_ps[g] = psum_abstract.tile([P, GROUP, PLANES, 2 * HALF], BF16, name="abstract_ps")
+                abstract_ps[g] = psum.tile([P, GROUP, PLANES, 2 * HALF], BF16, name="bank")
             for j in tiles:
                 nc.tensor.matmul(
                     out=abstract_ps[g][:, j, :, :].rearrange("p u w -> p (u w)"),
@@ -137,7 +135,7 @@ def tile_abstraction_pb_t_kernel(tc, data, pooled, W_abs, W_merge_words, W_merge
         def transpose_x(g):
             grouped_sb[g] = grouped_pool.tile([P, GROUP, P, 4], BF16, align_bytes=64, name="grouped")
             for half in range(GROUP // PER_BANK):
-                x_t_ps[g] = psum_x_t.tile([P, PER_BANK, PLANES, P], F32, name="x_t_ps")
+                x_t_ps[g] = psum.tile([P, PER_BANK, PLANES, P], F32, name="bank")
                 for j in range(PER_BANK):
                     for u in range(PLANES):
                         nc.tensor.transpose(
@@ -160,7 +158,7 @@ def tile_abstraction_pb_t_kernel(tc, data, pooled, W_abs, W_merge_words, W_merge
             )
 
         def merge_passes(g, half):
-            out_ps[g, half] = psum_out.tile([P, PER_BANK, D], F32, name="out_ps")
+            out_ps[g, half] = psum.tile([P, PER_BANK, D], F32, name="bank")
             for j in range(PER_BANK):
                 tokens = slice(P * (PER_BANK * half + j), P * (PER_BANK * half + j + 1))
                 nc.tensor.matmul_mx(

@@ -20,8 +20,14 @@ PLANES = 2
 J = 8
 N_CHUNKS = TOKENS // (P * J)
 GROUP = 4
-N_GROUPS = TOKENS // (P * GROUP)
-GROUPS_PER_CHUNK = J // GROUP
+SMALL_GROUP = 2
+SMALL_GROUPS_AT_AN_END = 2
+GROUP_TILES = (
+    [SMALL_GROUP] * SMALL_GROUPS_AT_AN_END
+    + [GROUP] * ((TOKENS // P - 2 * SMALL_GROUPS_AT_AN_END * SMALL_GROUP) // GROUP)
+    + [SMALL_GROUP] * SMALL_GROUPS_AT_AN_END
+)
+N_GROUPS = len(GROUP_TILES)
 PER_BANK = 2
 PSUM_BANKS = 8
 SORT_LAG = 1
@@ -99,27 +105,28 @@ def tile_abstraction_pb_t_kernel(tc, data, pooled, W_abs, W_merge_words, W_merge
         out_sb = {}
 
         def chunk_and_first_tile(g):
-            return g // GROUPS_PER_CHUNK, GROUP * (g % GROUPS_PER_CHUNK)
+            first = sum(GROUP_TILES[:g])
+            return first // J, first % J
 
         def transpose_pooled(g):
             c, j0 = chunk_and_first_tile(g)
-            pooled_t_ps[g] = psum.tile([A, GROUP, P], BF16, name="bank")
-            for j in range(GROUP):
+            pooled_t_ps[g] = psum.tile([A, GROUP_TILES[g], P], BF16, name="bank")
+            for j in range(GROUP_TILES[g]):
                 nc.tensor.transpose(pooled_t_ps[g][:, j, :], pooled_sb[c][:, j0 + j, :], ident_bf16[:])
-            pooled_t_sb[g] = pooled_t_pool.tile([A, GROUP, P], BF16, name="pooled_t")
+            pooled_t_sb[g] = pooled_t_pool.tile([A, GROUP_TILES[g], P], BF16, name="pooled_t")
             nc.scalar.copy(out=pooled_t_sb[g][:], in_=pooled_t_ps[g][:])
 
         def sort_data(g):
             c, j0 = chunk_and_first_tile(g)
-            x_sb[g] = x_pool.tile([P, GROUP, PLANES, 2 * P], BF16, name="x")
+            x_sb[g] = x_pool.tile([P, GROUP_TILES[g], PLANES, 2 * P], BF16, name="x")
             nc.vector.tensor_copy(
                 out=x_sb[g][:].bitcast(F32)[:, :, :, 0:HALF],
-                in_=data_sb[c][:].bitcast(F32)[:, j0 : j0 + GROUP, :].rearrange("p j (i u) -> p j u i", u=PLANES),
+                in_=data_sb[c][:].bitcast(F32)[:, j0 : j0 + GROUP_TILES[g], :].rearrange("p j (i u) -> p j u i", u=PLANES),
             )
 
         def abstract_matmuls(g, tiles):
             if g not in abstract_ps:
-                abstract_ps[g] = psum.tile([P, GROUP, PLANES, 2 * HALF], BF16, name="bank")
+                abstract_ps[g] = psum.tile([P, GROUP_TILES[g], PLANES, 2 * HALF], BF16, name="bank")
             for j in tiles:
                 nc.tensor.matmul(
                     out=abstract_ps[g][:, j, :, :].rearrange("p u w -> p (u w)"),
@@ -133,8 +140,8 @@ def tile_abstraction_pb_t_kernel(tc, data, pooled, W_abs, W_merge_words, W_merge
             nc.scalar.copy(out=x_sb[g][:, :, :, 2 * HALF : 4 * HALF], in_=abstract_ps[g][:])
 
         def transpose_x(g):
-            grouped_sb[g] = grouped_pool.tile([P, GROUP, P, 4], BF16, align_bytes=64, name="grouped")
-            for half in range(GROUP // PER_BANK):
+            grouped_sb[g] = grouped_pool.tile([P, GROUP_TILES[g], P, 4], BF16, align_bytes=64, name="grouped")
+            for half in range(GROUP_TILES[g] // PER_BANK):
                 x_t_ps[g] = psum.tile([P, PER_BANK, PLANES, P], F32, name="bank")
                 for j in range(PER_BANK):
                     for u in range(PLANES):
@@ -149,8 +156,8 @@ def tile_abstraction_pb_t_kernel(tc, data, pooled, W_abs, W_merge_words, W_merge
                 )
 
         def quantise(g):
-            codes_sb[g] = codes_pool.tile([P, GROUP * P], U32, align_bytes=64, name="codes")
-            scales_sb[g] = codes_pool.tile([P, GROUP * P], U8, align_bytes=64, name="scales")
+            codes_sb[g] = codes_pool.tile([P, GROUP_TILES[g] * P], U32, align_bytes=64, name="codes")
+            scales_sb[g] = codes_pool.tile([P, GROUP_TILES[g] * P], U8, align_bytes=64, name="scales")
             nc.vector.quantize_mx(
                 out=codes_sb[g][:].bitcast(FP8X4),
                 scales=scales_sb[g][:],
@@ -173,12 +180,12 @@ def tile_abstraction_pb_t_kernel(tc, data, pooled, W_abs, W_merge_words, W_merge
 
         def out_of_psum(g, half):
             if g not in out_sb:
-                out_sb[g] = out_pool.tile([P, GROUP, D], F32, name="out_g")
+                out_sb[g] = out_pool.tile([P, GROUP_TILES[g], D], F32, name="out_g")
             nc.scalar.copy(out=out_sb[g][:, PER_BANK * half : PER_BANK * (half + 1), :], in_=out_ps[g, half][:])
 
         def store(g):
             c, j0 = chunk_and_first_tile(g)
-            nc.sync.dma_start(out=out_chunks[c, :, j0 : j0 + GROUP, :], in_=out_sb[g][:])
+            nc.sync.dma_start(out=out_chunks[c, :, j0 : j0 + GROUP_TILES[g], :], in_=out_sb[g][:])
 
         def in_range(g):
             return 0 <= g < N_GROUPS
@@ -187,16 +194,18 @@ def tile_abstraction_pb_t_kernel(tc, data, pooled, W_abs, W_merge_words, W_merge
             g_abstract = step - ABSTRACT_LAG
             g_merge = step - MERGE_LAG
             if in_range(g_abstract):
-                abstract_matmuls(g_abstract, (0, 1))
+                abstract_matmuls(g_abstract, range(0, GROUP_TILES[g_abstract] // 2))
             if in_range(g_merge):
-                merge_passes(g_merge, 0)
-                out_of_psum(g_merge, 0)
-                merge_passes(g_merge, 1)
+                banks = GROUP_TILES[g_merge] // PER_BANK
+                for half in range(banks):
+                    merge_passes(g_merge, half)
+                    if half < banks - 1:
+                        out_of_psum(g_merge, half)
             if in_range(g_abstract):
-                abstract_matmuls(g_abstract, (2, 3))
+                abstract_matmuls(g_abstract, range(GROUP_TILES[g_abstract] // 2, GROUP_TILES[g_abstract]))
                 abstract_to_x(g_abstract)
             if in_range(g_merge):
-                out_of_psum(g_merge, 1)
+                out_of_psum(g_merge, banks - 1)
                 store(g_merge)
             if in_range(step - SORT_LAG):
                 sort_data(step - SORT_LAG)

@@ -29,7 +29,6 @@ GROUP_TILES = (
 )
 N_GROUPS = len(GROUP_TILES)
 PER_BANK = 2
-PSUM_BANKS = 8
 SORT_LAG = 1
 ABSTRACT_LAG = 2
 TRANSPOSE_LAG = 3
@@ -54,7 +53,10 @@ def tile_abstraction_pb_t_kernel(tc, data, pooled, W_abs, W_merge_words, W_merge
         grouped_pool = ctx.enter_context(tc.tile_pool(name="grouped", bufs=3))
         codes_pool = ctx.enter_context(tc.tile_pool(name="codes", bufs=4))
         out_pool = ctx.enter_context(tc.tile_pool(name="out", bufs=16))
-        psum = ctx.enter_context(tc.psum_pool(name="psum", bufs=PSUM_BANKS))
+        psum_pooled_t = ctx.enter_context(tc.psum_pool(name="psum_pooled_t", bufs=1))
+        psum_abstract = ctx.enter_context(tc.psum_pool(name="psum_abstract", bufs=2))
+        psum_x_t = ctx.enter_context(tc.psum_pool(name="psum_x_t", bufs=2))
+        psum_out = ctx.enter_context(tc.psum_pool(name="psum_out", bufs=3))
 
         ident_bf16 = consts.tile([P, P], BF16)
         make_identity(nc, ident_bf16[:])
@@ -110,7 +112,7 @@ def tile_abstraction_pb_t_kernel(tc, data, pooled, W_abs, W_merge_words, W_merge
 
         def transpose_pooled(g):
             c, j0 = chunk_and_first_tile(g)
-            pooled_t_ps[g] = psum.tile([A, GROUP_TILES[g], P], BF16, name="bank")
+            pooled_t_ps[g] = psum_pooled_t.tile([A, GROUP_TILES[g], P], BF16, name="pooled_t_ps")
             for j in range(GROUP_TILES[g]):
                 nc.tensor.transpose(pooled_t_ps[g][:, j, :], pooled_sb[c][:, j0 + j, :], ident_bf16[:])
             pooled_t_sb[g] = pooled_t_pool.tile([A, GROUP_TILES[g], P], BF16, name="pooled_t")
@@ -126,7 +128,7 @@ def tile_abstraction_pb_t_kernel(tc, data, pooled, W_abs, W_merge_words, W_merge
 
         def abstract_matmuls(g, tiles):
             if g not in abstract_ps:
-                abstract_ps[g] = psum.tile([P, GROUP_TILES[g], PLANES, 2 * HALF], BF16, name="bank")
+                abstract_ps[g] = psum_abstract.tile([P, GROUP_TILES[g], PLANES, 2 * HALF], BF16, name="abstract_ps")
             for j in tiles:
                 nc.tensor.matmul(
                     out=abstract_ps[g][:, j, :, :].rearrange("p u w -> p (u w)"),
@@ -142,7 +144,7 @@ def tile_abstraction_pb_t_kernel(tc, data, pooled, W_abs, W_merge_words, W_merge
         def transpose_x(g):
             grouped_sb[g] = grouped_pool.tile([P, GROUP_TILES[g], P, 4], BF16, align_bytes=64, name="grouped")
             for half in range(GROUP_TILES[g] // PER_BANK):
-                x_t_ps[g] = psum.tile([P, PER_BANK, PLANES, P], F32, name="bank")
+                x_t_ps[g] = psum_x_t.tile([P, PER_BANK, PLANES, P], F32, name="x_t_ps")
                 for j in range(PER_BANK):
                     for u in range(PLANES):
                         nc.tensor.transpose(
@@ -165,7 +167,7 @@ def tile_abstraction_pb_t_kernel(tc, data, pooled, W_abs, W_merge_words, W_merge
             )
 
         def merge_passes(g, half):
-            out_ps[g, half] = psum.tile([P, PER_BANK, D], F32, name="bank")
+            out_ps[g, half] = psum_out.tile([P, PER_BANK, D], F32, name="out_ps")
             for j in range(PER_BANK):
                 tokens = slice(P * (PER_BANK * half + j), P * (PER_BANK * half + j + 1))
                 nc.tensor.matmul_mx(

@@ -21,7 +21,7 @@ J = 8
 N_CHUNKS = TOKENS // (P * J)
 GROUP = 4
 SMALL_GROUP = 2
-SMALL_GROUPS_AT_AN_END = 2
+SMALL_GROUPS_AT_AN_END = 4
 GROUP_TILES = (
     [SMALL_GROUP] * SMALL_GROUPS_AT_AN_END
     + [GROUP] * ((TOKENS // P - 2 * SMALL_GROUPS_AT_AN_END * SMALL_GROUP) // GROUP)
@@ -68,17 +68,17 @@ def tile_abstraction_pb_t_kernel(tc, data, pooled, W_abs, W_merge_words, W_merge
         data_sb = {}
         pooled_sb = {}
 
-        def load_chunk(c):
-            pooled_c = inputs.tile([P, J, A], BF16, name="pooled%d" % c)
-            nc.sync.dma_start(out=pooled_c[:], in_=pooled_chunks[c])
-            pooled_sb[c] = pooled_c
-            data_c = inputs.tile([P, J, D], BF16, name="data%d" % c)
-            nc.sync.dma_start(out=data_c[:], in_=data_chunks[c])
-            data_sb[c] = data_c
+        def load_chunk(c, cuts):
+            pooled_sb[c] = inputs.tile([P, J, A], BF16, name="pooled%d" % c)
+            data_sb[c] = inputs.tile([P, J, D], BF16, name="data%d" % c)
+            for j0, j1 in zip(cuts[:-1], cuts[1:]):
+                nc.sync.dma_start(out=pooled_sb[c][:, j0:j1, :], in_=pooled_chunks[c, :, j0:j1, :])
+                if c == 0 and j0 == 0:
+                    nc.sync.dma_start(out=w_abs_raw[:], in_=W_abs)
+                nc.sync.dma_start(out=data_sb[c][:, j0:j1, :], in_=data_chunks[c, :, j0:j1, :])
 
         w_abs_raw = consts.tile([A, D], BF16)
-        nc.sync.dma_start(out=w_abs_raw[:], in_=W_abs)
-        load_chunk(0)
+        load_chunk(0, (0, GROUP_TILES[0], J))
         w_words = consts.tile([P, 2 * D], U8, align_bytes=64)
         nc.sync.dma_start(out=w_words[:].bitcast(I32), in_=W_merge_words[0].bitcast(I32))
         for quadrant in range(4):
@@ -87,7 +87,7 @@ def tile_abstraction_pb_t_kernel(tc, data, pooled, W_abs, W_merge_words, W_merge
                 in_=W_merge_scales[0, 4 * quadrant : 4 * quadrant + 4, :].bitcast(I32),
             )
         for c in range(1, N_CHUNKS):
-            load_chunk(c)
+            load_chunk(c, (0, J))
 
         w_abs = consts.tile([A, PLANES, HALF, 2], BF16)
         nc.vector.tensor_copy(

@@ -28,6 +28,7 @@ GROUP_TILES = (
     + [SMALL_GROUP] * SMALL_GROUPS_AT_AN_END
 )
 N_GROUPS = len(GROUP_TILES)
+SCALAR_SHARE = 5
 PER_BANK = 2
 SORT_LAG = 1
 ABSTRACT_LAG = 2
@@ -143,7 +144,8 @@ def tile_abstraction_pb_t_kernel(tc, data, pooled, W_abs, W_merge_words, W_merge
 
         def transpose_x(g):
             grouped_sb[g] = grouped_pool.tile([P, GROUP_TILES[g], P, 4], BF16, align_bytes=64, name="grouped")
-            for half in range(GROUP_TILES[g] // PER_BANK):
+            banks = GROUP_TILES[g] // PER_BANK
+            for half in range(banks):
                 x_t_ps[g] = psum_x_t.tile([P, PER_BANK, PLANES, P], F32, name="x_t_ps")
                 for j in range(PER_BANK):
                     for u in range(PLANES):
@@ -152,7 +154,8 @@ def tile_abstraction_pb_t_kernel(tc, data, pooled, W_abs, W_merge_words, W_merge
                             x_sb[g][:].bitcast(F32)[:, PER_BANK * half + j, u, :],
                             ident_f32[:],
                         )
-                nc.vector.tensor_copy(
+                on_scalar = banks > 1 and half == banks - 1 and g % SCALAR_SHARE == 0
+                (nc.scalar.copy if on_scalar else nc.vector.tensor_copy)(
                     out=grouped_sb[g][:].bitcast(F32)[:, PER_BANK * half : PER_BANK * (half + 1), :, :],
                     in_=x_t_ps[g][:].rearrange("p j u r -> p j r u"),
                 )

@@ -30,6 +30,8 @@ GROUP_TILES = (
 N_GROUPS = len(GROUP_TILES)
 SCALAR_SHARE = 5
 PER_BANK = 2
+WARM_BEFORE = 11
+WARM_AFTER_STEP = {0: 4, 2: 4}
 SORT_LAG = 1
 ABSTRACT_LAG = 2
 TRANSPOSE_LAG = 3
@@ -59,6 +61,8 @@ def tile_abstraction_pb_t_kernel(tc, data, pooled, W_abs, W_merge_words, W_merge
         psum_x_t = ctx.enter_context(tc.psum_pool(name="psum_x_t", bufs=2))
         psum_out = ctx.enter_context(tc.psum_pool(name="psum_out", bufs=3))
 
+        zeros = consts.tile([P, P], BF16)
+        nc.vector.memset(zeros[:], 0.0)
         ident_bf16 = consts.tile([P, P], BF16)
         make_identity(nc, ident_bf16[:])
         ident_f32 = consts.tile([P, P], F32)
@@ -95,6 +99,14 @@ def tile_abstraction_pb_t_kernel(tc, data, pooled, W_abs, W_merge_words, W_merge
             out=w_abs[:].bitcast(F32),
             in_=w_abs_raw[:].bitcast(F32).rearrange("a (i u) -> a u i", u=PLANES).unsqueeze(3),
         )
+
+        warm_ps = psum_out.tile([P, PER_BANK, D], F32, name="out_ps")
+
+        def keep_warm(count):
+            for i in range(count):
+                nc.tensor.matmul(out=warm_ps[:, 0, 0:P], lhsT=zeros[:], rhs=zeros[:], start=True, stop=True)
+
+        keep_warm(WARM_BEFORE)
 
         pooled_t_ps = {}
         pooled_t_sb = {}
@@ -220,3 +232,4 @@ def tile_abstraction_pb_t_kernel(tc, data, pooled, W_abs, W_merge_words, W_merge
                 transpose_x(step - TRANSPOSE_LAG)
             if in_range(step):
                 transpose_pooled(step)
+            keep_warm(WARM_AFTER_STEP.get(step, 0))

@@ -20,18 +20,18 @@ PLANES = 2
 J = 8
 N_CHUNKS = TOKENS // (P * J)
 GROUP = 4
-SMALL_GROUP = 2
-SMALL_GROUPS_AT_AN_END = 4
+FIRST_GROUPS = [2, 2, 2, 2]
+LAST_GROUPS = [2, 2, 2, 1, 1]
 GROUP_TILES = (
-    [SMALL_GROUP] * SMALL_GROUPS_AT_AN_END
-    + [GROUP] * ((TOKENS // P - 2 * SMALL_GROUPS_AT_AN_END * SMALL_GROUP) // GROUP)
-    + [SMALL_GROUP] * SMALL_GROUPS_AT_AN_END
+    FIRST_GROUPS
+    + [GROUP] * ((TOKENS // P - sum(FIRST_GROUPS) - sum(LAST_GROUPS)) // GROUP)
+    + LAST_GROUPS
 )
 N_GROUPS = len(GROUP_TILES)
 SCALAR_SHARE = 5
 PER_BANK = 2
 WARM_BEFORE = 11
-WARM_AFTER_STEP = {0: 4, 2: 4}
+WARM_AFTER_STEP = {0: 4}
 SORT_LAG = 1
 ABSTRACT_LAG = 2
 TRANSPOSE_LAG = 3
@@ -73,17 +73,28 @@ def tile_abstraction_pb_t_kernel(tc, data, pooled, W_abs, W_merge_words, W_merge
         data_sb = {}
         pooled_sb = {}
 
-        def load_chunk(c, cuts):
-            pooled_sb[c] = inputs.tile([P, J, A], BF16, name="pooled%d" % c)
-            data_sb[c] = inputs.tile([P, J, D], BF16, name="data%d" % c)
-            for j0, j1 in zip(cuts[:-1], cuts[1:]):
-                nc.sync.dma_start(out=pooled_sb[c][:, j0:j1, :], in_=pooled_chunks[c, :, j0:j1, :])
-                if c == 0 and j0 == 0:
-                    nc.sync.dma_start(out=w_abs_raw[:], in_=W_abs)
-                nc.sync.dma_start(out=data_sb[c][:, j0:j1, :], in_=data_chunks[c, :, j0:j1, :])
+        def load_pooled(c, j0, j1):
+            if c not in pooled_sb:
+                pooled_sb[c] = inputs.tile([P, J, A], BF16, name="pooled%d" % c)
+            nc.sync.dma_start(out=pooled_sb[c][:, j0:j1, :], in_=pooled_chunks[c, :, j0:j1, :])
+
+        def load_data(c, j0, j1):
+            if c not in data_sb:
+                data_sb[c] = inputs.tile([P, J, D], BF16, name="data%d" % c)
+            nc.sync.dma_start(out=data_sb[c][:, j0:j1, :], in_=data_chunks[c, :, j0:j1, :])
+
+        def load_chunk(c):
+            load_pooled(c, 0, J)
+            load_data(c, 0, J)
 
         w_abs_raw = consts.tile([A, D], BF16)
-        load_chunk(0, (0, GROUP_TILES[0], J))
+        cut = GROUP_TILES[0]
+        load_pooled(0, 0, cut)
+        load_pooled(0, cut, J)
+        nc.sync.dma_start(out=w_abs_raw[:], in_=W_abs)
+        load_data(0, 0, cut)
+        load_data(0, cut, J)
+        load_chunk(1)
         w_words = consts.tile([P, 2 * D], U8, align_bytes=64)
         nc.sync.dma_start(out=w_words[:].bitcast(I32), in_=W_merge_words[0].bitcast(I32))
         for quadrant in range(4):
@@ -91,8 +102,8 @@ def tile_abstraction_pb_t_kernel(tc, data, pooled, W_abs, W_merge_words, W_merge
                 out=w_scales[32 * quadrant : 32 * quadrant + 4, :].bitcast(I32),
                 in_=W_merge_scales[0, 4 * quadrant : 4 * quadrant + 4, :].bitcast(I32),
             )
-        for c in range(1, N_CHUNKS):
-            load_chunk(c, (0, J))
+        for c in range(2, N_CHUNKS):
+            load_chunk(c)
 
         w_abs = consts.tile([A, PLANES, HALF, 2], BF16)
         nc.vector.tensor_copy(
@@ -118,6 +129,10 @@ def tile_abstraction_pb_t_kernel(tc, data, pooled, W_abs, W_merge_words, W_merge
         scales_sb = {}
         out_ps = {}
         out_sb = {}
+
+        def banks_of(g):
+            n = GROUP_TILES[g]
+            return [range(first, min(first + PER_BANK, n)) for first in range(0, n, PER_BANK)]
 
         def chunk_and_first_tile(g):
             first = sum(GROUP_TILES[:g])
@@ -156,19 +171,19 @@ def tile_abstraction_pb_t_kernel(tc, data, pooled, W_abs, W_merge_words, W_merge
 
         def transpose_x(g):
             grouped_sb[g] = grouped_pool.tile([P, GROUP_TILES[g], P, 4], BF16, align_bytes=64, name="grouped")
-            banks = GROUP_TILES[g] // PER_BANK
-            for half in range(banks):
-                x_t_ps[g] = psum_x_t.tile([P, PER_BANK, PLANES, P], F32, name="x_t_ps")
-                for j in range(PER_BANK):
+            banks = banks_of(g)
+            for half, tiles in enumerate(banks):
+                x_t_ps[g] = psum_x_t.tile([P, len(tiles), PLANES, P], F32, name="x_t_ps")
+                for j in tiles:
                     for u in range(PLANES):
                         nc.tensor.transpose(
-                            x_t_ps[g][:, j, u, :],
-                            x_sb[g][:].bitcast(F32)[:, PER_BANK * half + j, u, :],
+                            x_t_ps[g][:, j - tiles.start, u, :],
+                            x_sb[g][:].bitcast(F32)[:, j, u, :],
                             ident_f32[:],
                         )
-                on_scalar = banks > 1 and half == banks - 1 and g % SCALAR_SHARE == 0
+                on_scalar = len(banks) > 1 and half == len(banks) - 1 and g % SCALAR_SHARE == 0
                 (nc.scalar.copy if on_scalar else nc.vector.tensor_copy)(
-                    out=grouped_sb[g][:].bitcast(F32)[:, PER_BANK * half : PER_BANK * (half + 1), :, :],
+                    out=grouped_sb[g][:].bitcast(F32)[:, tiles.start : tiles.stop, :, :],
                     in_=x_t_ps[g][:].rearrange("p j u r -> p j r u"),
                 )
 
@@ -182,11 +197,12 @@ def tile_abstraction_pb_t_kernel(tc, data, pooled, W_abs, W_merge_words, W_merge
             )
 
         def merge_passes(g, half):
-            out_ps[g, half] = psum_out.tile([P, PER_BANK, D], F32, name="out_ps")
-            for j in range(PER_BANK):
-                tokens = slice(P * (PER_BANK * half + j), P * (PER_BANK * half + j + 1))
+            tiles = banks_of(g)[half]
+            out_ps[g, half] = psum_out.tile([P, len(tiles), D], F32, name="out_ps")
+            for j in tiles:
+                tokens = slice(P * j, P * (j + 1))
                 nc.tensor.matmul_mx(
-                    out=out_ps[g, half][:, j, :],
+                    out=out_ps[g, half][:, j - tiles.start, :],
                     lhsT=codes_sb[g][:, tokens].bitcast(FP8X4),
                     lhsT_scale=scales_sb[g][:, tokens],
                     rhs=w_words[:].bitcast(FP4X4),
@@ -198,7 +214,8 @@ def tile_abstraction_pb_t_kernel(tc, data, pooled, W_abs, W_merge_words, W_merge
         def out_of_psum(g, half):
             if g not in out_sb:
                 out_sb[g] = out_pool.tile([P, GROUP_TILES[g], D], F32, name="out_g")
-            nc.scalar.copy(out=out_sb[g][:, PER_BANK * half : PER_BANK * (half + 1), :], in_=out_ps[g, half][:])
+            tiles = banks_of(g)[half]
+            nc.scalar.copy(out=out_sb[g][:, tiles.start : tiles.stop, :], in_=out_ps[g, half][:])
 
         def store(g):
             c, j0 = chunk_and_first_tile(g)
@@ -213,7 +230,7 @@ def tile_abstraction_pb_t_kernel(tc, data, pooled, W_abs, W_merge_words, W_merge
             if in_range(g_abstract):
                 abstract_matmuls(g_abstract, range(0, GROUP_TILES[g_abstract] // 2))
             if in_range(g_merge):
-                banks = GROUP_TILES[g_merge] // PER_BANK
+                banks = len(banks_of(g_merge))
                 for half in range(banks):
                     merge_passes(g_merge, half)
                     if half < banks - 1:

@@ -29,6 +29,7 @@ GROUP_TILES = (
 )
 N_GROUPS = len(GROUP_TILES)
 SCALAR_SHARE = 5
+EXCHANGED_GROUPS = 4
 PER_BANK = 2
 WARM_BEFORE = 11
 WARM_AFTER_STEP = {0: 4}
@@ -134,6 +135,16 @@ def tile_abstraction_pb_t_kernel(tc, data, pooled, W_abs, W_merge_words, W_merge
             n = GROUP_TILES[g]
             return [range(first, min(first + PER_BANK, n)) for first in range(0, n, PER_BANK)]
 
+        def x_t_on_scalar(g, half):
+            share = GROUP_TILES[g] == GROUP and half == 1 and g % SCALAR_SHARE == 0
+            return share or g >= N_GROUPS - EXCHANGED_GROUPS
+
+        def out_on_vector(g, half):
+            last_full = N_GROUPS - len(LAST_GROUPS) - 1
+            if GROUP_TILES[g] == GROUP:
+                return half == 1 and g > last_full - 2
+            return g >= N_GROUPS - EXCHANGED_GROUPS and (N_GROUPS - g) % 2 == 0
+
         def chunk_and_first_tile(g):
             first = sum(GROUP_TILES[:g])
             return first // J, first % J
@@ -181,8 +192,7 @@ def tile_abstraction_pb_t_kernel(tc, data, pooled, W_abs, W_merge_words, W_merge
                             x_sb[g][:].bitcast(F32)[:, j, u, :],
                             ident_f32[:],
                         )
-                on_scalar = len(banks) > 1 and half == len(banks) - 1 and g % SCALAR_SHARE == 0
-                (nc.scalar.copy if on_scalar else nc.vector.tensor_copy)(
+                (nc.scalar.copy if x_t_on_scalar(g, half) else nc.vector.tensor_copy)(
                     out=grouped_sb[g][:].bitcast(F32)[:, tiles.start : tiles.stop, :, :],
                     in_=x_t_ps[g][:].rearrange("p j u r -> p j r u"),
                 )
@@ -215,7 +225,9 @@ def tile_abstraction_pb_t_kernel(tc, data, pooled, W_abs, W_merge_words, W_merge
             if g not in out_sb:
                 out_sb[g] = out_pool.tile([P, GROUP_TILES[g], D], F32, name="out_g")
             tiles = banks_of(g)[half]
-            nc.scalar.copy(out=out_sb[g][:, tiles.start : tiles.stop, :], in_=out_ps[g, half][:])
+            (nc.vector.tensor_copy if out_on_vector(g, half) else nc.scalar.copy)(
+                out=out_sb[g][:, tiles.start : tiles.stop, :], in_=out_ps[g, half][:]
+            )
 
         def store(g):
             c, j0 = chunk_and_first_tile(g)

@@ -30,6 +30,7 @@ GROUP_TILES = (
 N_GROUPS = len(GROUP_TILES)
 SCALAR_SHARE = 5
 EXCHANGED_GROUPS = 4
+ALIGN = 256
 PER_BANK = 2
 WARM_BEFORE = 11
 WARM_AFTER_STEP = {0: 4}
@@ -62,13 +63,13 @@ def tile_abstraction_pb_t_kernel(tc, data, pooled, W_abs, W_merge_words, W_merge
         psum_x_t = ctx.enter_context(tc.psum_pool(name="psum_x_t", bufs=2))
         psum_out = ctx.enter_context(tc.psum_pool(name="psum_out", bufs=3))
 
-        zeros = consts.tile([P, P], BF16)
+        zeros = consts.tile([P, P], BF16, align_bytes=ALIGN)
         nc.vector.memset(zeros[:], 0.0)
-        ident_bf16 = consts.tile([P, P], BF16)
+        ident_bf16 = consts.tile([P, P], BF16, align_bytes=ALIGN)
         make_identity(nc, ident_bf16[:])
-        ident_f32 = consts.tile([P, P], F32)
+        ident_f32 = consts.tile([P, P], F32, align_bytes=ALIGN)
         make_identity(nc, ident_f32[:])
-        w_scales = consts.tile([P, D], U8, align_bytes=64)
+        w_scales = consts.tile([P, D], U8, align_bytes=ALIGN)
         nc.vector.memset(w_scales[:].bitcast(I32), 0)
 
         data_sb = {}
@@ -76,19 +77,19 @@ def tile_abstraction_pb_t_kernel(tc, data, pooled, W_abs, W_merge_words, W_merge
 
         def load_pooled(c, j0, j1):
             if c not in pooled_sb:
-                pooled_sb[c] = inputs.tile([P, J, A], BF16, name="pooled%d" % c)
+                pooled_sb[c] = inputs.tile([P, J, A], BF16, name="pooled%d" % c, align_bytes=ALIGN)
             nc.sync.dma_start(out=pooled_sb[c][:, j0:j1, :], in_=pooled_chunks[c, :, j0:j1, :])
 
         def load_data(c, j0, j1):
             if c not in data_sb:
-                data_sb[c] = inputs.tile([P, J, D], BF16, name="data%d" % c)
+                data_sb[c] = inputs.tile([P, J, D], BF16, name="data%d" % c, align_bytes=ALIGN)
             nc.sync.dma_start(out=data_sb[c][:, j0:j1, :], in_=data_chunks[c, :, j0:j1, :])
 
         def load_chunk(c):
             load_pooled(c, 0, J)
             load_data(c, 0, J)
 
-        w_abs_raw = consts.tile([A, D], BF16)
+        w_abs_raw = consts.tile([A, D], BF16, align_bytes=ALIGN)
         cut = GROUP_TILES[0]
         load_pooled(0, 0, cut)
         load_pooled(0, cut, J)
@@ -96,7 +97,7 @@ def tile_abstraction_pb_t_kernel(tc, data, pooled, W_abs, W_merge_words, W_merge
         load_data(0, 0, cut)
         load_data(0, cut, J)
         load_chunk(1)
-        w_words = consts.tile([P, 2 * D], U8, align_bytes=64)
+        w_words = consts.tile([P, 2 * D], U8, align_bytes=ALIGN)
         nc.sync.dma_start(out=w_words[:].bitcast(I32), in_=W_merge_words[0].bitcast(I32))
         for quadrant in range(4):
             nc.sync.dma_start(
@@ -106,7 +107,7 @@ def tile_abstraction_pb_t_kernel(tc, data, pooled, W_abs, W_merge_words, W_merge
         for c in range(2, N_CHUNKS):
             load_chunk(c)
 
-        w_abs = consts.tile([A, PLANES, HALF, 2], BF16)
+        w_abs = consts.tile([A, PLANES, HALF, 2], BF16, align_bytes=ALIGN)
         nc.vector.tensor_copy(
             out=w_abs[:].bitcast(F32),
             in_=w_abs_raw[:].bitcast(F32).rearrange("a (i u) -> a u i", u=PLANES).unsqueeze(3),
@@ -154,12 +155,12 @@ def tile_abstraction_pb_t_kernel(tc, data, pooled, W_abs, W_merge_words, W_merge
             pooled_t_ps[g] = psum_pooled_t.tile([A, GROUP_TILES[g], P], BF16, name="pooled_t_ps")
             for j in range(GROUP_TILES[g]):
                 nc.tensor.transpose(pooled_t_ps[g][:, j, :], pooled_sb[c][:, j0 + j, :], ident_bf16[:])
-            pooled_t_sb[g] = pooled_t_pool.tile([A, GROUP_TILES[g], P], BF16, name="pooled_t")
+            pooled_t_sb[g] = pooled_t_pool.tile([A, GROUP_TILES[g], P], BF16, name="pooled_t", align_bytes=ALIGN)
             nc.scalar.copy(out=pooled_t_sb[g][:], in_=pooled_t_ps[g][:])
 
         def sort_data(g):
             c, j0 = chunk_and_first_tile(g)
-            x_sb[g] = x_pool.tile([P, GROUP_TILES[g], PLANES, 2 * P], BF16, name="x")
+            x_sb[g] = x_pool.tile([P, GROUP_TILES[g], PLANES, 2 * P], BF16, name="x", align_bytes=ALIGN)
             nc.vector.tensor_copy(
                 out=x_sb[g][:].bitcast(F32)[:, :, :, 0:HALF],
                 in_=data_sb[c][:].bitcast(F32)[:, j0 : j0 + GROUP_TILES[g], :].rearrange("p j (i u) -> p j u i", u=PLANES),
@@ -181,7 +182,7 @@ def tile_abstraction_pb_t_kernel(tc, data, pooled, W_abs, W_merge_words, W_merge
             nc.scalar.copy(out=x_sb[g][:, :, :, 2 * HALF : 4 * HALF], in_=abstract_ps[g][:])
 
         def transpose_x(g):
-            grouped_sb[g] = grouped_pool.tile([P, GROUP_TILES[g], P, 4], BF16, align_bytes=64, name="grouped")
+            grouped_sb[g] = grouped_pool.tile([P, GROUP_TILES[g], P, 4], BF16, align_bytes=ALIGN, name="grouped")
             banks = banks_of(g)
             for half, tiles in enumerate(banks):
                 x_t_ps[g] = psum_x_t.tile([P, len(tiles), PLANES, P], F32, name="x_t_ps")
@@ -198,8 +199,8 @@ def tile_abstraction_pb_t_kernel(tc, data, pooled, W_abs, W_merge_words, W_merge
                 )
 
         def quantise(g):
-            codes_sb[g] = codes_pool.tile([P, GROUP_TILES[g] * P], U32, align_bytes=64, name="codes")
-            scales_sb[g] = codes_pool.tile([P, GROUP_TILES[g] * P], U8, align_bytes=64, name="scales")
+            codes_sb[g] = codes_pool.tile([P, GROUP_TILES[g] * P], U32, align_bytes=ALIGN, name="codes")
+            scales_sb[g] = codes_pool.tile([P, GROUP_TILES[g] * P], U8, align_bytes=ALIGN, name="scales")
             nc.vector.quantize_mx(
                 out=codes_sb[g][:].bitcast(FP8X4),
                 scales=scales_sb[g][:],
@@ -223,7 +224,7 @@ def tile_abstraction_pb_t_kernel(tc, data, pooled, W_abs, W_merge_words, W_merge
 
         def out_of_psum(g, half):
             if g not in out_sb:
-                out_sb[g] = out_pool.tile([P, GROUP_TILES[g], D], F32, name="out_g")
+                out_sb[g] = out_pool.tile([P, GROUP_TILES[g], D], F32, name="out_g", align_bytes=ALIGN)
             tiles = banks_of(g)[half]
             (nc.vector.tensor_copy if out_on_vector(g, half) else nc.scalar.copy)(
                 out=out_sb[g][:, tiles.start : tiles.stop, :], in_=out_ps[g, half][:]

@@ -33,7 +33,7 @@ EXCHANGED_GROUPS = 4
 ALIGN = 256
 PER_BANK = 2
 WARM_BEFORE = 11
-WARM_AFTER_STEP = {0: 4}
+WARM_LATER = 4
 SORT_LAG = 1
 ABSTRACT_LAG = 2
 TRANSPOSE_LAG = 3
@@ -152,7 +152,10 @@ def tile_abstraction_pb_t_kernel(tc, data, pooled, W_abs, W_merge_words, W_merge
 
         def transpose_pooled(g):
             c, j0 = chunk_and_first_tile(g)
-            pooled_t_ps[g] = psum_pooled_t.tile([A, GROUP_TILES[g], P], BF16, name="pooled_t_ps")
+            if 0 < g < len(FIRST_GROUPS):
+                pooled_t_ps[g] = psum_out.tile([A, GROUP_TILES[g], P], BF16, name="out_ps")
+            else:
+                pooled_t_ps[g] = psum_pooled_t.tile([A, GROUP_TILES[g], P], BF16, name="pooled_t_ps")
             for j in range(GROUP_TILES[g]):
                 nc.tensor.transpose(pooled_t_ps[g][:, j, :], pooled_sb[c][:, j0 + j, :], ident_bf16[:])
             pooled_t_sb[g] = pooled_t_pool.tile([A, GROUP_TILES[g], P], BF16, name="pooled_t", align_bytes=ALIGN)
@@ -258,8 +261,11 @@ def tile_abstraction_pb_t_kernel(tc, data, pooled, W_abs, W_merge_words, W_merge
                 sort_data(step - SORT_LAG)
             if in_range(step - QUANTISE_LAG):
                 quantise(step - QUANTISE_LAG)
+            if step == TRANSPOSE_LAG:
+                keep_warm(WARM_LATER)
             if in_range(step - TRANSPOSE_LAG):
                 transpose_x(step - TRANSPOSE_LAG)
             if in_range(step):
                 transpose_pooled(step)
-            keep_warm(WARM_AFTER_STEP.get(step, 0))
+            if step == 0:
+                keep_warm(WARM_LATER)

from contextlib import ExitStack

import concourse.mybir as mybir
from concourse.masks import make_identity

BF16 = mybir.dt.bfloat16
F32 = mybir.dt.float32
I32 = mybir.dt.int32
U8 = mybir.dt.uint8
U32 = mybir.dt.uint32
FP8X4 = mybir.dt.float8_e4m3fn_x4
FP4X4 = mybir.dt.float4_e2m1fn_x4

P = 128
TOKENS = 4 * 4096
D = 256
A = 128
HALF = D // 4
PLANES = 2
J = 8
N_CHUNKS = TOKENS // (P * J)
GROUP = 4
FIRST_GROUPS = [2, 2, 2, 2]
LAST_GROUPS = [2, 2, 2, 1, 1]
GROUP_TILES = (
    FIRST_GROUPS
    + [GROUP] * ((TOKENS // P - sum(FIRST_GROUPS) - sum(LAST_GROUPS)) // GROUP)
    + LAST_GROUPS
)
N_GROUPS = len(GROUP_TILES)
SCALAR_SHARE = 5
EXCHANGED_GROUPS = 4
ALIGN = 256
PER_BANK = 2
WARM_BEFORE = 11
WARM_LATER = 4
SORT_LAG = 1
ABSTRACT_LAG = 2
TRANSPOSE_LAG = 3
QUANTISE_LAG = 4
MERGE_LAG = 6

FLOPS = 2 * TOKENS * A * D + 2 * TOKENS * (2 * D) * D


def tile_abstraction_pb_t_kernel(tc, data, pooled, W_abs, W_merge_words, W_merge_scales, out):
    nc = tc.nc
    data_chunks = data.flatten_outer_dims().rearrange("(c p j) d -> c p j d", p=P, j=J)
    pooled_chunks = pooled.flatten_outer_dims().rearrange("(c p j) a -> c p j a", p=P, j=J)
    out_chunks = out.flatten_outer_dims().rearrange("(c p j) n -> c p j n", p=P, j=J)

    with ExitStack() as ctx:
        ctx.enter_context(tc.manual_schedule())
        consts = ctx.enter_context(tc.tile_pool(name="consts", bufs=1))
        inputs = ctx.enter_context(tc.tile_pool(name="inputs", bufs=1))
        pooled_t_pool = ctx.enter_context(tc.tile_pool(name="pooled_t", bufs=4))
        x_pool = ctx.enter_context(tc.tile_pool(name="x", bufs=4))
        grouped_pool = ctx.enter_context(tc.tile_pool(name="grouped", bufs=3))
        codes_pool = ctx.enter_context(tc.tile_pool(name="codes", bufs=4))
        out_pool = ctx.enter_context(tc.tile_pool(name="out", bufs=16))
        psum_pooled_t = ctx.enter_context(tc.psum_pool(name="psum_pooled_t", bufs=1))
        psum_abstract = ctx.enter_context(tc.psum_pool(name="psum_abstract", bufs=2))
        psum_x_t = ctx.enter_context(tc.psum_pool(name="psum_x_t", bufs=2))
        psum_out = ctx.enter_context(tc.psum_pool(name="psum_out", bufs=3))

        zeros = consts.tile([P, P], BF16, align_bytes=ALIGN)
        nc.vector.memset(zeros[:], 0.0)
        ident_bf16 = consts.tile([P, P], BF16, align_bytes=ALIGN)
        make_identity(nc, ident_bf16[:])
        ident_f32 = consts.tile([P, P], F32, align_bytes=ALIGN)
        make_identity(nc, ident_f32[:])
        w_scales = consts.tile([P, D], U8, align_bytes=ALIGN)
        nc.vector.memset(w_scales[:].bitcast(I32), 0)

        data_sb = {}
        pooled_sb = {}

        def load_pooled(c, j0, j1):
            if c not in pooled_sb:
                pooled_sb[c] = inputs.tile([P, J, A], BF16, name="pooled%d" % c, align_bytes=ALIGN)
            nc.sync.dma_start(out=pooled_sb[c][:, j0:j1, :], in_=pooled_chunks[c, :, j0:j1, :])

        def load_data(c, j0, j1):
            if c not in data_sb:
                data_sb[c] = inputs.tile([P, J, D], BF16, name="data%d" % c, align_bytes=ALIGN)
            nc.sync.dma_start(out=data_sb[c][:, j0:j1, :], in_=data_chunks[c, :, j0:j1, :])

        def load_chunk(c):
            load_pooled(c, 0, J)
            load_data(c, 0, J)

        w_abs_raw = consts.tile([A, D], BF16, align_bytes=ALIGN)
        cut = GROUP_TILES[0]
        load_pooled(0, 0, cut)
        load_pooled(0, cut, J)
        nc.sync.dma_start(out=w_abs_raw[:], in_=W_abs)
        load_data(0, 0, cut)
        load_data(0, cut, J)
        load_chunk(1)
        w_words = consts.tile([P, 2 * D], U8, align_bytes=ALIGN)
        nc.sync.dma_start(out=w_words[:].bitcast(I32), in_=W_merge_words[0].bitcast(I32))
        for quadrant in range(4):
            nc.sync.dma_start(
                out=w_scales[32 * quadrant : 32 * quadrant + 4, :].bitcast(I32),
                in_=W_merge_scales[0, 4 * quadrant : 4 * quadrant + 4, :].bitcast(I32),
            )
        for c in range(2, N_CHUNKS):
            load_chunk(c)

        w_abs = consts.tile([A, PLANES, HALF, 2], BF16, align_bytes=ALIGN)
        nc.vector.tensor_copy(
            out=w_abs[:].bitcast(F32),
            in_=w_abs_raw[:].bitcast(F32).rearrange("a (i u) -> a u i", u=PLANES).unsqueeze(3),
        )

        warm_ps = psum_out.tile([P, PER_BANK, D], F32, name="out_ps")

        def keep_warm(count):
            for i in range(count):
                nc.tensor.matmul(out=warm_ps[:, 0, 0:P], lhsT=zeros[:], rhs=zeros[:], start=True, stop=True)

        keep_warm(WARM_BEFORE)

        pooled_t_ps = {}
        pooled_t_sb = {}
        x_sb = {}
        abstract_ps = {}
        x_t_ps = {}
        grouped_sb = {}
        codes_sb = {}
        scales_sb = {}
        out_ps = {}
        out_sb = {}

        def banks_of(g):
            n = GROUP_TILES[g]
            return [range(first, min(first + PER_BANK, n)) for first in range(0, n, PER_BANK)]

        def x_t_on_scalar(g, half):
            share = GROUP_TILES[g] == GROUP and half == 1 and g % SCALAR_SHARE == 0
            return share or g >= N_GROUPS - EXCHANGED_GROUPS

        def out_on_vector(g, half):
            last_full = N_GROUPS - len(LAST_GROUPS) - 1
            if GROUP_TILES[g] == GROUP:
                return half == 1 and g > last_full - 2
            return g >= N_GROUPS - EXCHANGED_GROUPS and (N_GROUPS - g) % 2 == 0

        def chunk_and_first_tile(g):
            first = sum(GROUP_TILES[:g])
            return first // J, first % J

        def transpose_pooled(g):
            c, j0 = chunk_and_first_tile(g)
            if 0 < g < len(FIRST_GROUPS):
                pooled_t_ps[g] = psum_out.tile([A, GROUP_TILES[g], P], BF16, name="out_ps")
            else:
                pooled_t_ps[g] = psum_pooled_t.tile([A, GROUP_TILES[g], P], BF16, name="pooled_t_ps")
            for j in range(GROUP_TILES[g]):
                nc.tensor.transpose(pooled_t_ps[g][:, j, :], pooled_sb[c][:, j0 + j, :], ident_bf16[:])
            pooled_t_sb[g] = pooled_t_pool.tile([A, GROUP_TILES[g], P], BF16, name="pooled_t", align_bytes=ALIGN)
            nc.scalar.copy(out=pooled_t_sb[g][:], in_=pooled_t_ps[g][:])

        def sort_data(g):
            c, j0 = chunk_and_first_tile(g)
            x_sb[g] = x_pool.tile([P, GROUP_TILES[g], PLANES, 2 * P], BF16, name="x", align_bytes=ALIGN)
            nc.vector.tensor_copy(
                out=x_sb[g][:].bitcast(F32)[:, :, :, 0:HALF],
                in_=data_sb[c][:].bitcast(F32)[:, j0 : j0 + GROUP_TILES[g], :].rearrange("p j (i u) -> p j u i", u=PLANES),
            )

        def abstract_matmuls(g, tiles):
            if g not in abstract_ps:
                abstract_ps[g] = psum_abstract.tile([P, GROUP_TILES[g], PLANES, 2 * HALF], BF16, name="abstract_ps")
            for j in tiles:
                nc.tensor.matmul(
                    out=abstract_ps[g][:, j, :, :].rearrange("p u w -> p (u w)"),
                    lhsT=pooled_t_sb[g][:, j, :],
                    rhs=w_abs[:].rearrange("a u i e -> a (u i e)"),
                    start=True,
                    stop=True,
                )

        def abstract_to_x(g):
            nc.scalar.copy(out=x_sb[g][:, :, :, 2 * HALF : 4 * HALF], in_=abstract_ps[g][:])

        def transpose_x(g):
            grouped_sb[g] = grouped_pool.tile([P, GROUP_TILES[g], P, 4], BF16, align_bytes=ALIGN, name="grouped")
            banks = banks_of(g)
            for half, tiles in enumerate(banks):
                x_t_ps[g] = psum_x_t.tile([P, len(tiles), PLANES, P], F32, name="x_t_ps")
                for j in tiles:
                    for u in range(PLANES):
                        nc.tensor.transpose(
                            x_t_ps[g][:, j - tiles.start, u, :],
                            x_sb[g][:].bitcast(F32)[:, j, u, :],
                            ident_f32[:],
                        )
                (nc.scalar.copy if x_t_on_scalar(g, half) else nc.vector.tensor_copy)(
                    out=grouped_sb[g][:].bitcast(F32)[:, tiles.start : tiles.stop, :, :],
                    in_=x_t_ps[g][:].rearrange("p j u r -> p j r u"),
                )

        def quantise(g):
            codes_sb[g] = codes_pool.tile([P, GROUP_TILES[g] * P], U32, align_bytes=ALIGN, name="codes")
            scales_sb[g] = codes_pool.tile([P, GROUP_TILES[g] * P], U8, align_bytes=ALIGN, name="scales")
            nc.vector.quantize_mx(
                out=codes_sb[g][:].bitcast(FP8X4),
                scales=scales_sb[g][:],
                in_=grouped_sb[g][:].rearrange("p j r t -> p (j r t)"),
            )

        def merge_passes(g, half):
            tiles = banks_of(g)[half]
            out_ps[g, half] = psum_out.tile([P, len(tiles), D], F32, name="out_ps")
            for j in tiles:
                tokens = slice(P * j, P * (j + 1))
                nc.tensor.matmul_mx(
                    out=out_ps[g, half][:, j - tiles.start, :],
                    lhsT=codes_sb[g][:, tokens].bitcast(FP8X4),
                    lhsT_scale=scales_sb[g][:, tokens],
                    rhs=w_words[:].bitcast(FP4X4),
                    rhs_scale=w_scales[:],
                    start=True,
                    stop=True,
                )

        def out_of_psum(g, half):
            if g not in out_sb:
                out_sb[g] = out_pool.tile([P, GROUP_TILES[g], D], F32, name="out_g", align_bytes=ALIGN)
            tiles = banks_of(g)[half]
            (nc.vector.tensor_copy if out_on_vector(g, half) else nc.scalar.copy)(
                out=out_sb[g][:, tiles.start : tiles.stop, :], in_=out_ps[g, half][:]
            )

        def store(g):
            c, j0 = chunk_and_first_tile(g)
            nc.sync.dma_start(out=out_chunks[c, :, j0 : j0 + GROUP_TILES[g], :], in_=out_sb[g][:])

        def in_range(g):
            return 0 <= g < N_GROUPS

        for step in range(N_GROUPS + MERGE_LAG):
            g_abstract = step - ABSTRACT_LAG
            g_merge = step - MERGE_LAG
            if in_range(g_abstract):
                abstract_matmuls(g_abstract, range(0, GROUP_TILES[g_abstract] // 2))
            if in_range(g_merge):
                banks = len(banks_of(g_merge))
                for half in range(banks):
                    merge_passes(g_merge, half)
                    if half < banks - 1:
                        out_of_psum(g_merge, half)
            if in_range(g_abstract):
                abstract_matmuls(g_abstract, range(GROUP_TILES[g_abstract] // 2, GROUP_TILES[g_abstract]))
                abstract_to_x(g_abstract)
            if in_range(g_merge):
                out_of_psum(g_merge, banks - 1)
                store(g_merge)
            if in_range(step - SORT_LAG):
                sort_data(step - SORT_LAG)
            if in_range(step - QUANTISE_LAG):
                quantise(step - QUANTISE_LAG)
            if step == TRANSPOSE_LAG:
                keep_warm(WARM_LATER)
            if in_range(step - TRANSPOSE_LAG):
                transpose_x(step - TRANSPOSE_LAG)
            if in_range(step):
                transpose_pooled(step)
            if step == 0:
                keep_warm(WARM_LATER)
